import numpy as np
import ml_dtypes


def mxq(x, axis, fmt="e4m3"):
    dtype, down = {"e4m3": (ml_dtypes.float8_e4m3fn, 7), "e5m2": (ml_dtypes.float8_e5m2, 14)}[fmt]
    v = np.moveaxis(np.asarray(x, np.float32).astype(ml_dtypes.bfloat16).astype(np.float64), axis, -1)
    blocks = v.reshape(v.shape[:-1] + (-1, 32))
    amax = np.abs(blocks).max(-1, keepdims=True)
    byte = np.maximum(np.where(amax > 0, np.frexp(amax)[1] - 1 + 127, 0) - down, 1)
    scale = np.exp2(byte - 127.0)
    codes = (blocks / scale).astype(np.float32).astype(dtype).astype(np.float64)
    return np.moveaxis((codes * scale).reshape(v.shape), -1, axis)


WIDE = False


def mx_kscale(k):
    if not WIDE:
        return np.ones(k)
    levels = np.array([10, -10, 5, -5, 0])
    if k % 512:
        return np.exp2(np.random.permutation(np.resize(levels, k // 32))).repeat(32)
    a = np.empty((k // 512, 16))
    for p in range(k // 512):
        a[p, :8] = np.random.permutation(np.resize(levels, 8))
        for g in range(8):
            far = levels[np.abs(levels - a[p, g]) >= 10]
            a[p, g + 8] = far[np.random.randint(len(far))]
    return np.exp2(a.ravel()).repeat(32)


BF16 = ml_dtypes.bfloat16


def bf(x):
    return np.asarray(x, np.float32).astype(BF16)


def f64(x):
    return np.asarray(x).astype(np.float64)


S, E = 1536, 1024


def draw0():
    s, t = mx_kscale(E), mx_kscale(S)
    return {"qm": bf(np.random.standard_normal((S, E)) * 0.4 * s),
            "km": bf(np.random.standard_normal((S, E)) * 0.4 / s * t[:, None]),
            "vm": bf(np.random.standard_normal((S, E)) * 0.4 / t[:, None])}


def core(qm, km, vm):
    qkm = (mxq(f64(qm), 1, "e4m3") @ mxq(f64(km), 1, "e4m3").T) / np.sqrt(S)
    z = mxq(qkm, 1, "e4m3") @ mxq(f64(vm), 0, "e4m3")
    e = np.exp(z - z.max(-1, keepdims=True))
    return e / e.sum(-1, keepdims=True)


def e4m3fn_bytes(y):
    return np.clip(np.asarray(y, np.float64), -448.0, 448.0).astype(np.float32).astype(ml_dtypes.float8_e4m3fn).view(np.uint8)


def e4m3fn_values(b):
    return np.asarray(b, np.uint8).view(ml_dtypes.float8_e4m3fn).astype(np.float64)


def setup_inputs():
    d = draw0()
    x0 = np.asarray(d['vm']).astype(np.float64)
    s = (np.max(np.abs(x0), axis=(1,), keepdims=True) / 448.0).astype(np.float32)
    out = {}
    for k, v in d.items():
        if k == 'vm':
            out['vm_bytes'] = e4m3fn_bytes(x0 / s.astype(np.float64))
            out['vm_scale'] = s
        else:
            out[k] = v
    return out


def reference(qm, km, vm_bytes, vm_scale):
    return core(qm, km, e4m3fn_values(vm_bytes) * vm_scale.astype(np.float64))

@@ -1,0 +1,299 @@
+import math
+from contextlib import ExitStack
+
+import concourse.mybir as mybir
+from concourse.masks import make_identity
+
+S, E = 1536, 1024
+FLOPS = 2 * 2 * S * S * E
+
+F32 = mybir.dt.float32
+BF16 = mybir.dt.bfloat16
+U32 = mybir.dt.uint32
+U8 = mybir.dt.uint8
+FP8 = mybir.dt.float8_e4m3fn
+FP8X4 = mybir.dt.float8_e4m3fn_x4
+ACT = mybir.ActivationFunctionType
+ALU = mybir.AluOpType
+
+P = 128
+PACK = 4
+K_PASS = P * PACK
+BANK = 512
+E_PASSES = E // K_PASS
+S_PASSES = S // K_PASS
+TILES = S // P
+PAIRS = TILES // 2
+HALVES = E // BANK
+SPLIT = 576
+
+
+def tile_headattetion_pa_kernel(tc, qm, km, vm_bytes, vm_scale, out):
+    nc = tc.nc
+
+    q_pairs = qm.rearrange("(a p e) k -> a p (e k)", p=P, e=2)
+    k_pairs = km.rearrange("(g m h e) k -> g h m (e k)", m=P, h=2, e=2)
+    v_groups = vm_bytes.rearrange("(g p t) n -> g p (t n)", p=P, t=PACK)
+    out_tiles = out.rearrange("(a p e) n -> a e p n", p=P, e=2)
+
+    with ExitStack() as ctx:
+        keep = ctx.enter_context(tc.tile_pool(name="keep", bufs=1))
+        stage = ctx.enter_context(tc.tile_pool(name="stage", bufs=3))
+        psum = ctx.enter_context(tc.psum_pool(name="psum", bufs=4))
+        ctx.enter_context(tc.manual_schedule())
+
+        raw, turned, codes, scales = {}, {}, {}, {}
+        v_bytes, v_rows, v_woven = {}, {}, {}
+        score_bf, z_bank, z_neg, z_min, expo, total, inv = {}, {}, {}, {}, {}, {}, {}
+
+        v_scale = keep.tile([P, S_PASSES, PACK], F32, name="v_scale")
+        nc.scalar.dma_start(out=v_scale[:], in_=vm_scale.rearrange("(g p t) o -> p g (t o)", p=P, t=PACK))
+
+        def load_pair(key):
+            src = q_pairs[key[1]] if key[0] == "q" else k_pairs[key[1] // 2, key[1] % 2]
+            raw[key] = keep.tile([P, 2 * E], BF16, name="raw_%s%d" % key)
+            nc.sync.dma_start(out=raw[key][:], in_=src)
+
+        def load_v(g):
+            v_bytes[g] = keep.tile([P, PACK * E], U8, name="v_bytes%d" % g)
+            nc.sync.dma_start(out=v_bytes[g][:], in_=v_groups[g])
+
+        for key in (("q", 0), ("k", 0), ("k", 1), ("q", 1), ("k", 2)):
+            load_pair(key)
+        load_v(0)
+        for key in (("k", 3), ("k", 4), ("k", 5)):
+            load_pair(key)
+        load_v(1)
+        load_pair(("q", 2))
+        load_v(2)
+        for a in range(3, PAIRS):
+            load_pair(("q", a))
+
+        identity = keep.tile([P, P], F32, name="identity")
+        make_identity(nc, identity[:])
+
+        def quantize(key, source, width):
+            codes[key] = keep.tile([P, width], U32, name="codes_%s%d" % key, align_bytes=64)
+            scales[key] = keep.tile([P, width], U8, name="scales_%s%d" % key, align_bytes=64)
+            nc.vector.quantize_mx(out=codes[key][:].bitcast(FP8X4), scales=scales[key][:], in_=source)
+
+        def turn_pair(key, share_with_vector=False):
+            words = raw[key][:].bitcast(F32)
+            turned[key] = stage.tile([P, 2 * E], BF16, name="turned", align_bytes=64)
+            for e in range(2):
+                bank = psum.tile([P, 2 * E_PASSES, P], F32, name="bank")
+                for j in range(E_PASSES):
+                    first = (e * E_PASSES + j) * 2 * P
+                    for u in range(2):
+                        nc.tensor.transpose(bank[:, 2 * j + u, :], words[:, first + u : first + 2 * P : 2], identity[:])
+                dst = turned[key][:, e * E : (e + 1) * E]
+                if key == ("q", 0) and e == 0:
+                    nc.scalar.activation(
+                        out=dst.rearrange("p (j r u c) -> p j r u c", j=E_PASSES, u=2, c=2)[:, 0],
+                        in_=bank[:, 0:2, :].bitcast(BF16).rearrange("p u (r c) -> p r u c", c=2),
+                        func=ACT.Copy,
+                    )
+                    nc.scalar.copy(
+                        out=dst.bitcast(F32).rearrange("p (j r u) -> p j r u", j=E_PASSES, u=2)[:, 1],
+                        in_=bank[:, 2:4, :].rearrange("p u r -> p r u"),
+                    )
+                    continue
+                dst_words = dst.bitcast(F32).rearrange("p (j r u) -> p j r u", j=E_PASSES, u=2)
+                src_words = bank[:].rearrange("p (j u) r -> p j r u", u=2)
+                if share_with_vector and e == 1:
+                    nc.vector.tensor_copy(out=dst_words, in_=src_words)
+                else:
+                    nc.scalar.copy(out=dst_words, in_=src_words)
+
+        def quantize_pair(key):
+            quantize(key, turned[key][:], 2 * E // PACK)
+
+        def scores(i, g):
+            if g == 0:
+                score_bf[i] = stage.tile([P, S], BF16, name="score_bf", bufs=8, align_bytes=64)
+            bank = psum.tile([P, PACK, P], F32, name="bank")
+            q_key = ("q", i // 2)
+            for t in range(PACK):
+                k_key = ("k", 2 * g + t // 2)
+                for j in range(E_PASSES):
+                    k_cols = slice(((t % 2) * E_PASSES + j) * P, ((t % 2) * E_PASSES + j + 1) * P)
+                    q_cols = slice(((i % 2) * E_PASSES + j) * P, ((i % 2) * E_PASSES + j + 1) * P)
+                    nc.tensor.matmul_mx(
+                        out=bank[:, t, :],
+                        lhsT=codes[k_key][:, k_cols].bitcast(FP8X4),
+                        lhsT_scale=scales[k_key][:, k_cols],
+                        rhs=codes[q_key][:, q_cols].bitcast(FP8X4),
+                        rhs_scale=scales[q_key][:, q_cols],
+                        start=(j == 0),
+                        stop=(j == E_PASSES - 1),
+                    )
+            nc.scalar.activation(
+                out=score_bf[i][:, g * K_PASS : (g + 1) * K_PASS].rearrange("p (q t) -> p q t", t=PACK),
+                in_=bank[:].rearrange("p t q -> p q t"),
+                func=ACT.Copy,
+                scale=1.0 / math.sqrt(S),
+            )
+
+        def quantize_scores(i):
+            quantize(("s", i), score_bf[i][:], S // PACK)
+
+        def widen_v(n):
+            g, h = divmod(n, HALVES)
+            v_rows[n] = stage.tile([P, PACK, BANK], BF16, name="v_rows")
+            for t in range(PACK):
+                first = t * E + h * BANK
+                nc.vector.tensor_scalar(
+                    out=v_rows[n][:, t, :],
+                    in0=v_bytes[g][:, first : first + BANK].bitcast(FP8),
+                    scalar1=v_scale[:, g, t : t + 1],
+                    scalar2=None,
+                    op0=ALU.mult,
+                )
+
+        def weave_v(n):
+            v_woven[n] = stage.tile([P, BANK * PACK], BF16, name="v_woven", align_bytes=64)
+            nc.vector.tensor_copy(
+                out=v_woven[n][:].rearrange("p (c i t) -> p c t i", i=4, t=PACK),
+                in_=v_rows[n][:].rearrange("p t (c i) -> p c t i", i=4),
+            )
+
+        def quantize_v(n):
+            quantize(("v", n), v_woven[n][:], BANK)
+
+        def mix(i, h):
+            z_bank[i, h] = psum.tile([P, BANK], F32, name="z_bank")
+            for g in range(S_PASSES):
+                cols = slice(g * P, (g + 1) * P)
+                v_key = ("v", g * HALVES + h)
+                nc.tensor.matmul_mx(
+                    out=z_bank[i, h][:],
+                    lhsT=codes["s", i][:, cols].bitcast(FP8X4),
+                    lhsT_scale=scales["s", i][:, cols],
+                    rhs=codes[v_key][:].bitcast(FP8X4),
+                    rhs_scale=scales[v_key][:],
+                    start=(g == 0),
+                    stop=(g == S_PASSES - 1),
+                )
+
+        def negate_and_min(i, h):
+            if h == 0:
+                z_neg[i] = stage.tile([P, E], F32, name="z_neg")
+            z_min[i, h] = stage.tile([P, 1], F32, name="z_min", bufs=6)
+            nc.vector.tensor_scalar(
+                out=z_neg[i][:, h * BANK : (h + 1) * BANK],
+                in0=z_bank[i, h][:],
+                scalar1=-1.0,
+                scalar2=z_min[i, h - 1][:] if h else None,
+                op0=ALU.mult,
+                op1=ALU.min,
+                accum_out=z_min[i, h][:],
+            )
+
+        def exponentiate(i):
+            expo[i] = stage.tile([P, E], F32, name="expo", bufs=4)
+            total[i] = stage.tile([P, 1], F32, name="total", bufs=4)
+            nc.scalar.activation(
+                out=expo[i][:],
+                in_=z_neg[i][:],
+                func=ACT.Exp,
+                scale=-1.0,
+                bias=z_min[i, HALVES - 1][:],
+                accum_out=total[i][:],
+            )
+
+        def invert(i):
+            inv[i] = stage.tile([P, 1], F32, name="inv", bufs=4)
+            nc.vector.reciprocal(out=inv[i][:], in_=total[i][:])
+
+        def normalize(i, share_with_scalar):
+            rows = out_tiles[i // 2, i % 2]
+            split = SPLIT if share_with_scalar else E
+            left = expo[i][:, :split]
+            nc.vector.tensor_scalar(out=left, in0=left, scalar1=inv[i][:], scalar2=None, op0=ALU.mult)
+            nc.sync.dma_start(out=rows[:, :split], in_=left)
+            if share_with_scalar:
+                right = expo[i][:, split:]
+                nc.scalar.activation(out=right, in_=right, func=ACT.Copy, scale=inv[i][:])
+                nc.sync.dma_start(out=rows[:, split:], in_=right)
+
+        turn_pair(("q", 0), True)
+        turn_pair(("k", 0), True)
+        quantize_pair(("q", 0))
+        turn_pair(("k", 1), True)
+        quantize_pair(("k", 0))
+        turn_pair(("q", 1))
+        quantize_pair(("k", 1))
+        turn_pair(("k", 2))
+        quantize_pair(("q", 1))
+        widen_v(0)
+        for i in range(4):
+            scores(i, 0)
+        quantize_pair(("k", 2))
+        widen_v(1)
+        weave_v(0)
+        turn_pair(("k", 3))
+        turn_pair(("k", 4))
+        quantize_pair(("k", 3))
+        weave_v(1)
+        turn_pair(("k", 5))
+        quantize_v(0)
+        quantize_pair(("k", 4))
+        quantize_v(1)
+        quantize_pair(("k", 5))
+        for i in range(4):
+            scores(i, 1)
+        widen_v(2)
+        widen_v(3)
+        turn_pair(("q", 2))
+        turn_pair(("q", 3))
+        weave_v(2)
+        quantize_pair(("q", 2))
+        weave_v(3)
+        quantize_v(2)
+        quantize_pair(("q", 3))
+        quantize_v(3)
+        for i in range(4):
+            scores(i, 2)
+        widen_v(4)
+        widen_v(5)
+        weave_v(4)
+        weave_v(5)
+        for i in range(4, 6):
+            for g in range(S_PASSES):
+                scores(i, g)
+        turn_pair(("q", 4))
+        turn_pair(("q", 5))
+        quantize_scores(0)
+        quantize_v(4)
+        quantize_v(5)
+        for i in range(6, 8):
+            for g in range(S_PASSES):
+                scores(i, g)
+        quantize_scores(1)
+        quantize_pair(("q", 4))
+        quantize_scores(2)
+        quantize_pair(("q", 5))
+
+        todo = [(i, g) for i in range(8, TILES) for g in range(S_PASSES)]
+        scored, quantized = 8, 3
+        for i in range(TILES):
+            mix(i, 0)
+            mix(i, 1)
+            negate_and_min(i, 0)
+            if i >= 2:
+                normalize(i - 2, not todo)
+            negate_and_min(i, 1)
+            take = 2 if i < 4 else 1
+            for n, g in todo[:take]:
+                scores(n, g)
+                scored = n + (g + 1) // S_PASSES
+            todo = todo[take:]
+            exponentiate(i)
+            if i >= 1:
+                invert(i - 1)
+            for n in range(quantized, min(quantized + 2, scored)):
+                quantize_scores(n)
+                quantized = n + 1
+        normalize(TILES - 2, False)
+        invert(TILES - 1)
+        normalize(TILES - 1, True)

@@ -25,7 +25,7 @@ S_PASSES = S // K_PASS
 TILES = S // P
 PAIRS = TILES // 2
 HALVES = E // BANK
-SPLIT = 576
+SPLIT = 704
 
 
 def tile_headattetion_pa_kernel(tc, qm, km, vm_bytes, vm_scale, out):
@@ -39,10 +39,10 @@ def tile_headattetion_pa_kernel(tc, qm, km, vm_bytes, vm_scale, out):
     with ExitStack() as ctx:
         keep = ctx.enter_context(tc.tile_pool(name="keep", bufs=1))
         stage = ctx.enter_context(tc.tile_pool(name="stage", bufs=3))
-        psum = ctx.enter_context(tc.psum_pool(name="psum", bufs=4))
+        psum = ctx.enter_context(tc.psum_pool(name="psum", bufs=8))
         ctx.enter_context(tc.manual_schedule())
 
-        raw, turned, codes, scales = {}, {}, {}, {}
+        raw, lined, turned, codes, scales = {}, {}, {}, {}, {}
         v_bytes, v_rows, v_woven = {}, {}, {}
         score_bf, z_bank, z_neg, z_min, expo, total, inv = {}, {}, {}, {}, {}, {}, {}
 
@@ -51,7 +51,7 @@ def tile_headattetion_pa_kernel(tc, qm, km, vm_bytes, vm_scale, out):
 
         def load_pair(key):
             src = q_pairs[key[1]] if key[0] == "q" else k_pairs[key[1] // 2, key[1] % 2]
-            raw[key] = keep.tile([P, 2 * E], BF16, name="raw_%s%d" % key)
+            raw[key] = stage.tile([P, 2 * E], BF16, name="raw", tag="raw", bufs=8)
             nc.sync.dma_start(out=raw[key][:], in_=src)
 
         def load_v(g):
@@ -63,11 +63,6 @@ def tile_headattetion_pa_kernel(tc, qm, km, vm_bytes, vm_scale, out):
         load_v(0)
         for key in (("k", 3), ("k", 4), ("k", 5)):
             load_pair(key)
-        load_v(1)
-        load_pair(("q", 2))
-        load_v(2)
-        for a in range(3, PAIRS):
-            load_pair(("q", a))
 
         identity = keep.tile([P, P], F32, name="identity")
         make_identity(nc, identity[:])
@@ -77,6 +72,13 @@ def tile_headattetion_pa_kernel(tc, qm, km, vm_bytes, vm_scale, out):
             scales[key] = keep.tile([P, width], U8, name="scales_%s%d" % key, align_bytes=64)
             nc.vector.quantize_mx(out=codes[key][:].bitcast(FP8X4), scales=scales[key][:], in_=source)
 
+        def line_up(key):
+            lined[key] = stage.tile([P, E], F32, name="lined")
+            nc.vector.tensor_copy(
+                out=lined[key][:].rearrange("p (s u w) -> p s u w", u=2, w=P),
+                in_=raw[key][:].bitcast(F32).rearrange("p (s w u) -> p s u w", u=2, w=P),
+            )
+
         def turn_pair(key, share_with_vector=False):
             words = raw[key][:].bitcast(F32)
             turned[key] = stage.tile([P, 2 * E], BF16, name="turned", align_bytes=64)
@@ -85,7 +87,11 @@ def tile_headattetion_pa_kernel(tc, qm, km, vm_bytes, vm_scale, out):
                 for j in range(E_PASSES):
                     first = (e * E_PASSES + j) * 2 * P
                     for u in range(2):
-                        nc.tensor.transpose(bank[:, 2 * j + u, :], words[:, first + u : first + 2 * P : 2], identity[:])
+                        if key in lined:
+                            src = lined[key][:, first + u * P : first + (u + 1) * P]
+                        else:
+                            src = words[:, first + u : first + 2 * P : 2]
+                        nc.tensor.transpose(bank[:, 2 * j + u, :], src, identity[:])
                 dst = turned[key][:, e * E : (e + 1) * E]
                 if key == ("q", 0) and e == 0:
                     nc.scalar.activation(
@@ -110,7 +116,7 @@ def tile_headattetion_pa_kernel(tc, qm, km, vm_bytes, vm_scale, out):
 
         def scores(i, g):
             if g == 0:
-                score_bf[i] = stage.tile([P, S], BF16, name="score_bf", bufs=8, align_bytes=64)
+                score_bf[i] = stage.tile([P, S], BF16, name="score_bf", bufs=12, align_bytes=64)
             bank = psum.tile([P, PACK, P], F32, name="bank")
             q_key = ("q", i // 2)
             for t in range(PACK):
@@ -161,7 +167,7 @@ def tile_headattetion_pa_kernel(tc, qm, km, vm_bytes, vm_scale, out):
             quantize(("v", n), v_woven[n][:], BANK)
 
         def mix(i, h):
-            z_bank[i, h] = psum.tile([P, BANK], F32, name="z_bank")
+            z_bank[i, h] = psum.tile([P, BANK], F32, name="bank")
             for g in range(S_PASSES):
                 cols = slice(g * P, (g + 1) * P)
                 v_key = ("v", g * HALVES + h)
@@ -190,8 +196,8 @@ def tile_headattetion_pa_kernel(tc, qm, km, vm_bytes, vm_scale, out):
             )
 
         def exponentiate(i):
-            expo[i] = stage.tile([P, E], F32, name="expo", bufs=4)
-            total[i] = stage.tile([P, 1], F32, name="total", bufs=4)
+            expo[i] = stage.tile([P, E], F32, name="expo", tag="raw", bufs=8)
+            total[i] = stage.tile([P, 1], F32, name="total", bufs=6)
             nc.scalar.activation(
                 out=expo[i][:],
                 in_=z_neg[i][:],
@@ -202,14 +208,17 @@ def tile_headattetion_pa_kernel(tc, qm, km, vm_bytes, vm_scale, out):
             )
 
         def invert(i):
-            inv[i] = stage.tile([P, 1], F32, name="inv", bufs=4)
+            inv[i] = stage.tile([P, 1], F32, name="inv", bufs=6)
             nc.vector.reciprocal(out=inv[i][:], in_=total[i][:])
 
-        def normalize(i, share_with_scalar):
+        def normalize(i, on_vector, share_with_scalar):
             rows = out_tiles[i // 2, i % 2]
             split = SPLIT if share_with_scalar else E
             left = expo[i][:, :split]
-            nc.vector.tensor_scalar(out=left, in0=left, scalar1=inv[i][:], scalar2=None, op0=ALU.mult)
+            if on_vector:
+                nc.vector.tensor_scalar(out=left, in0=left, scalar1=inv[i][:], scalar2=None, op0=ALU.mult)
+            else:
+                nc.gpsimd.tensor_scalar(out=left, in0=left, scalar1=inv[i][:], scalar2=0.0, op0=ALU.mult, op1=ALU.add)
             nc.sync.dma_start(out=rows[:, :split], in_=left)
             if share_with_scalar:
                 right = expo[i][:, split:]
@@ -217,11 +226,17 @@ def tile_headattetion_pa_kernel(tc, qm, km, vm_bytes, vm_scale, out):
                 nc.sync.dma_start(out=rows[:, split:], in_=right)
 
         turn_pair(("q", 0), True)
+        load_pair(("q", 2))
         turn_pair(("k", 0), True)
+        load_pair(("q", 3))
+        load_v(1)
         quantize_pair(("q", 0))
         turn_pair(("k", 1), True)
+        load_pair(("q", 4))
         quantize_pair(("k", 0))
         turn_pair(("q", 1))
+        load_pair(("q", 5))
+        load_v(2)
         quantize_pair(("k", 1))
         turn_pair(("k", 2))
         quantize_pair(("q", 1))
@@ -229,71 +244,78 @@ def tile_headattetion_pa_kernel(tc, qm, km, vm_bytes, vm_scale, out):
         for i in range(4):
             scores(i, 0)
         quantize_pair(("k", 2))
-        widen_v(1)
         weave_v(0)
+        line_up(("k", 5))
         turn_pair(("k", 3))
         turn_pair(("k", 4))
-        quantize_pair(("k", 3))
-        weave_v(1)
         turn_pair(("k", 5))
         quantize_v(0)
+        quantize_pair(("k", 3))
+        line_up(("q", 2))
         quantize_pair(("k", 4))
-        quantize_v(1)
-        quantize_pair(("k", 5))
+        line_up(("q", 3))
         for i in range(4):
             scores(i, 1)
-        widen_v(2)
-        widen_v(3)
+        quantize_pair(("k", 5))
         turn_pair(("q", 2))
         turn_pair(("q", 3))
-        weave_v(2)
-        quantize_pair(("q", 2))
-        weave_v(3)
-        quantize_v(2)
-        quantize_pair(("q", 3))
-        quantize_v(3)
+        widen_v(1)
+        widen_v(2)
         for i in range(4):
             scores(i, 2)
-        widen_v(4)
-        widen_v(5)
-        weave_v(4)
-        weave_v(5)
+        quantize_pair(("q", 2))
+        weave_v(1)
+        line_up(("q", 4))
+        quantize_v(1)
+        line_up(("q", 5))
+        weave_v(2)
+        quantize_pair(("q", 3))
         for i in range(4, 6):
             for g in range(S_PASSES):
                 scores(i, g)
         turn_pair(("q", 4))
         turn_pair(("q", 5))
-        quantize_scores(0)
+        widen_v(3)
+        quantize_v(2)
+        weave_v(3)
+        widen_v(4)
+        quantize_pair(("q", 4))
+        quantize_v(3)
+        quantize_pair(("q", 5))
+        weave_v(4)
+        widen_v(5)
         quantize_v(4)
+        weave_v(5)
+        quantize_scores(0)
         quantize_v(5)
-        for i in range(6, 8):
+        for i in range(6, 11):
             for g in range(S_PASSES):
                 scores(i, g)
         quantize_scores(1)
-        quantize_pair(("q", 4))
-        quantize_scores(2)
-        quantize_pair(("q", 5))
 
-        todo = [(i, g) for i in range(8, TILES) for g in range(S_PASSES)]
-        scored, quantized = 8, 3
+        todo = [(i, g) for i in range(11, TILES) for g in range(S_PASSES)]
+        for n in range(2, 4):
+            quantize_scores(n)
+        quantized, normalized = 4, 0
         for i in range(TILES):
             mix(i, 0)
             mix(i, 1)
             negate_and_min(i, 0)
-            if i >= 2:
-                normalize(i - 2, not todo)
+            busy = quantized < TILES
+            if busy:
+                for n in range(quantized, min(quantized + (2 if i < len(todo) else 1), TILES)):
+                    quantize_scores(n)
+                    quantized = n + 1
+                if i >= 2:
+                    invert(i - 2)
             negate_and_min(i, 1)
-            take = 2 if i < 4 else 1
-            for n, g in todo[:take]:
+            for n, g in todo[i : i + 1]:
                 scores(n, g)
-                scored = n + (g + 1) // S_PASSES
-            todo = todo[take:]
             exponentiate(i)
-            if i >= 1:
-                invert(i - 1)
-            for n in range(quantized, min(quantized + 2, scored)):
-                quantize_scores(n)
-                quantized = n + 1
-        normalize(TILES - 2, False)
+            for n in range(normalized, i - 1 if busy else i):
+                if not busy:
+                    invert(n)
+                normalize(n, n == TILES - 2, n < TILES - 2 and True)
+                normalized = n + 1
         invert(TILES - 1)
-        normalize(TILES - 1, True)
+        normalize(TILES - 1, True, True)

@@ -47,7 +47,6 @@ def tile_headattetion_pa_kernel(tc, qm, km, vm_bytes, vm_scale, out):
         score_bf, z_bank, z_neg, z_min, expo, total, inv = {}, {}, {}, {}, {}, {}, {}
 
         v_scale = keep.tile([P, S_PASSES, PACK], F32, name="v_scale")
-        nc.scalar.dma_start(out=v_scale[:], in_=vm_scale.rearrange("(g p t) o -> p g (t o)", p=P, t=PACK))
 
         def load_pair(key):
             src = q_pairs[key[1]] if key[0] == "q" else k_pairs[key[1] // 2, key[1] % 2]
@@ -60,6 +59,7 @@ def tile_headattetion_pa_kernel(tc, qm, km, vm_bytes, vm_scale, out):
 
         for key in (("q", 0), ("k", 0), ("k", 1), ("q", 1), ("k", 2)):
             load_pair(key)
+        nc.sync.dma_start(out=v_scale[:], in_=vm_scale.rearrange("(g p t) o -> p g (t o)", p=P, t=PACK))
         load_v(0)
         for key in (("k", 3), ("k", 4), ("k", 5)):
             load_pair(key)
@@ -241,34 +241,37 @@ def tile_headattetion_pa_kernel(tc, qm, km, vm_bytes, vm_scale, out):
         turn_pair(("k", 2))
         quantize_pair(("q", 1))
         widen_v(0)
-        for i in range(4):
-            scores(i, 0)
+        scores(0, 0)
+        scores(1, 0)
         quantize_pair(("k", 2))
-        weave_v(0)
-        line_up(("k", 5))
+        widen_v(1)
         turn_pair(("k", 3))
+        line_up(("k", 4))
+        scores(2, 0)
+        scores(3, 0)
+        line_up(("k", 5))
+        quantize_pair(("k", 3))
         turn_pair(("k", 4))
         turn_pair(("k", 5))
-        quantize_v(0)
-        quantize_pair(("k", 3))
+        weave_v(0)
         line_up(("q", 2))
-        quantize_pair(("k", 4))
         line_up(("q", 3))
         for i in range(4):
             scores(i, 1)
+        quantize_pair(("k", 4))
         quantize_pair(("k", 5))
         turn_pair(("q", 2))
         turn_pair(("q", 3))
-        widen_v(1)
+        weave_v(1)
+        quantize_v(0)
         widen_v(2)
+        quantize_pair(("q", 2))
         for i in range(4):
             scores(i, 2)
-        quantize_pair(("q", 2))
-        weave_v(1)
-        line_up(("q", 4))
         quantize_v(1)
-        line_up(("q", 5))
+        line_up(("q", 4))
         weave_v(2)
+        line_up(("q", 5))
         quantize_pair(("q", 3))
         for i in range(4, 6):
             for g in range(S_PASSES):

@@ -25,7 +25,8 @@ S_PASSES = S // K_PASS
 TILES = S // P
 PAIRS = TILES // 2
 HALVES = E // BANK
-SPLIT = 704
+SPLIT = 768
+LAST_SPLIT = 640
 
 
 def tile_headattetion_pa_kernel(tc, qm, km, vm_bytes, vm_scale, out):
@@ -47,19 +48,19 @@ def tile_headattetion_pa_kernel(tc, qm, km, vm_bytes, vm_scale, out):
         score_bf, z_bank, z_neg, z_min, expo, total, inv = {}, {}, {}, {}, {}, {}, {}
 
         v_scale = keep.tile([P, S_PASSES, PACK], F32, name="v_scale")
+        nc.scalar.dma_start(out=v_scale[:], in_=vm_scale.rearrange("(g p t) o -> p g (t o)", p=P, t=PACK))
 
         def load_pair(key):
             src = q_pairs[key[1]] if key[0] == "q" else k_pairs[key[1] // 2, key[1] % 2]
-            raw[key] = stage.tile([P, 2 * E], BF16, name="raw", tag="raw", bufs=8)
+            raw[key] = stage.tile([P, 2 * E], BF16, name="raw", tag="raw", bufs=8, align_bytes=256)
             nc.sync.dma_start(out=raw[key][:], in_=src)
 
         def load_v(g):
-            v_bytes[g] = keep.tile([P, PACK * E], U8, name="v_bytes%d" % g)
+            v_bytes[g] = keep.tile([P, PACK * E], U8, name="v_bytes%d" % g, align_bytes=256)
             nc.sync.dma_start(out=v_bytes[g][:], in_=v_groups[g])
 
         for key in (("q", 0), ("k", 0), ("k", 1), ("q", 1), ("k", 2)):
             load_pair(key)
-        nc.sync.dma_start(out=v_scale[:], in_=vm_scale.rearrange("(g p t) o -> p g (t o)", p=P, t=PACK))
         load_v(0)
         for key in (("k", 3), ("k", 4), ("k", 5)):
             load_pair(key)
@@ -196,7 +197,7 @@ def tile_headattetion_pa_kernel(tc, qm, km, vm_bytes, vm_scale, out):
             )
 
         def exponentiate(i):
-            expo[i] = stage.tile([P, E], F32, name="expo", tag="raw", bufs=8)
+            expo[i] = stage.tile([P, E], F32, name="expo", tag="raw", bufs=8, align_bytes=256)
             total[i] = stage.tile([P, 1], F32, name="total", bufs=6)
             nc.scalar.activation(
                 out=expo[i][:],
@@ -213,7 +214,7 @@ def tile_headattetion_pa_kernel(tc, qm, km, vm_bytes, vm_scale, out):
 
         def normalize(i, on_vector, share_with_scalar):
             rows = out_tiles[i // 2, i % 2]
-            split = SPLIT if share_with_scalar else E
+            split = (LAST_SPLIT if on_vector else SPLIT) if share_with_scalar else E
             left = expo[i][:, :split]
             if on_vector:
                 nc.vector.tensor_scalar(out=left, in0=left, scalar1=inv[i][:], scalar2=None, op0=ALU.mult)
@@ -304,21 +305,19 @@ def tile_headattetion_pa_kernel(tc, qm, km, vm_bytes, vm_scale, out):
             mix(i, 0)
             mix(i, 1)
             negate_and_min(i, 0)
-            busy = quantized < TILES
-            if busy:
-                for n in range(quantized, min(quantized + (2 if i < len(todo) else 1), TILES)):
-                    quantize_scores(n)
-                    quantized = n + 1
-                if i >= 2:
-                    invert(i - 2)
+            for n in range(quantized, min(quantized + (2 if i < len(todo) else 1), TILES)):
+                quantize_scores(n)
+                quantized = n + 1
+            if i >= 2 and normalized == i - 2:
+                invert(i - 2)
             negate_and_min(i, 1)
             for n, g in todo[i : i + 1]:
                 scores(n, g)
             exponentiate(i)
-            for n in range(normalized, i - 1 if busy else i):
-                if not busy:
+            for n in range(normalized, i - 1 if i < 9 else i):
+                if n == i - 1:
                     invert(n)
-                normalize(n, n == TILES - 2, n < TILES - 2 and True)
+                normalize(n, n >= TILES - 2, n < TILES - 2)
                 normalized = n + 1
         invert(TILES - 1)
         normalize(TILES - 1, True, True)

import math
from contextlib import ExitStack

import concourse.mybir as mybir
from concourse.masks import make_identity

S, E = 1536, 1024
FLOPS = 2 * 2 * S * S * E

F32 = mybir.dt.float32
BF16 = mybir.dt.bfloat16
U32 = mybir.dt.uint32
U8 = mybir.dt.uint8
FP8 = mybir.dt.float8_e4m3fn
FP8X4 = mybir.dt.float8_e4m3fn_x4
ACT = mybir.ActivationFunctionType
ALU = mybir.AluOpType

P = 128
PACK = 4
K_PASS = P * PACK
BANK = 512
E_PASSES = E // K_PASS
S_PASSES = S // K_PASS
TILES = S // P
PAIRS = TILES // 2
HALVES = E // BANK
SPLIT = 768
LAST_SPLIT = 640


def tile_headattetion_pa_kernel(tc, qm, km, vm_bytes, vm_scale, out):
    nc = tc.nc

    q_pairs = qm.rearrange("(a p e) k -> a p (e k)", p=P, e=2)
    k_pairs = km.rearrange("(g m h e) k -> g h m (e k)", m=P, h=2, e=2)
    v_groups = vm_bytes.rearrange("(g p t) n -> g p (t n)", p=P, t=PACK)
    out_tiles = out.rearrange("(a p e) n -> a e p n", p=P, e=2)

    with ExitStack() as ctx:
        keep = ctx.enter_context(tc.tile_pool(name="keep", bufs=1))
        stage = ctx.enter_context(tc.tile_pool(name="stage", bufs=3))
        psum = ctx.enter_context(tc.psum_pool(name="psum", bufs=8))
        ctx.enter_context(tc.manual_schedule())

        raw, lined, turned, codes, scales = {}, {}, {}, {}, {}
        v_bytes, v_rows, v_woven = {}, {}, {}
        score_bf, z_bank, z_neg, z_min, expo, total, inv = {}, {}, {}, {}, {}, {}, {}

        v_scale = keep.tile([P, S_PASSES, PACK], F32, name="v_scale")
        nc.scalar.dma_start(out=v_scale[:], in_=vm_scale.rearrange("(g p t) o -> p g (t o)", p=P, t=PACK))

        def load_pair(key):
            src = q_pairs[key[1]] if key[0] == "q" else k_pairs[key[1] // 2, key[1] % 2]
            raw[key] = stage.tile([P, 2 * E], BF16, name="raw", tag="raw", bufs=8, align_bytes=256)
            nc.sync.dma_start(out=raw[key][:], in_=src)

        def load_v(g):
            v_bytes[g] = keep.tile([P, PACK * E], U8, name="v_bytes%d" % g, align_bytes=256)
            nc.sync.dma_start(out=v_bytes[g][:], in_=v_groups[g])

        for key in (("q", 0), ("k", 0), ("k", 1), ("q", 1), ("k", 2)):
            load_pair(key)
        load_v(0)
        for key in (("k", 3), ("k", 4), ("k", 5)):
            load_pair(key)

        identity = keep.tile([P, P], F32, name="identity")
        make_identity(nc, identity[:])

        def quantize(key, source, width):
            codes[key] = keep.tile([P, width], U32, name="codes_%s%d" % key, align_bytes=64)
            scales[key] = keep.tile([P, width], U8, name="scales_%s%d" % key, align_bytes=64)
            nc.vector.quantize_mx(out=codes[key][:].bitcast(FP8X4), scales=scales[key][:], in_=source)

        def line_up(key):
            lined[key] = stage.tile([P, E], F32, name="lined")
            nc.vector.tensor_copy(
                out=lined[key][:].rearrange("p (s u w) -> p s u w", u=2, w=P),
                in_=raw[key][:].bitcast(F32).rearrange("p (s w u) -> p s u w", u=2, w=P),
            )

        def turn_pair(key, share_with_vector=False):
            words = raw[key][:].bitcast(F32)
            turned[key] = stage.tile([P, 2 * E], BF16, name="turned", align_bytes=64)
            for e in range(2):
                bank = psum.tile([P, 2 * E_PASSES, P], F32, name="bank")
                for j in range(E_PASSES):
                    first = (e * E_PASSES + j) * 2 * P
                    for u in range(2):
                        if key in lined:
                            src = lined[key][:, first + u * P : first + (u + 1) * P]
                        else:
                            src = words[:, first + u : first + 2 * P : 2]
                        nc.tensor.transpose(bank[:, 2 * j + u, :], src, identity[:])
                dst = turned[key][:, e * E : (e + 1) * E]
                if key == ("q", 0) and e == 0:
                    nc.scalar.activation(
                        out=dst.rearrange("p (j r u c) -> p j r u c", j=E_PASSES, u=2, c=2)[:, 0],
                        in_=bank[:, 0:2, :].bitcast(BF16).rearrange("p u (r c) -> p r u c", c=2),
                        func=ACT.Copy,
                    )
                    nc.scalar.copy(
                        out=dst.bitcast(F32).rearrange("p (j r u) -> p j r u", j=E_PASSES, u=2)[:, 1],
                        in_=bank[:, 2:4, :].rearrange("p u r -> p r u"),
                    )
                    continue
                dst_words = dst.bitcast(F32).rearrange("p (j r u) -> p j r u", j=E_PASSES, u=2)
                src_words = bank[:].rearrange("p (j u) r -> p j r u", u=2)
                if share_with_vector and e == 1:
                    nc.vector.tensor_copy(out=dst_words, in_=src_words)
                else:
                    nc.scalar.copy(out=dst_words, in_=src_words)

        def quantize_pair(key):
            quantize(key, turned[key][:], 2 * E // PACK)

        def scores(i, g):
            if g == 0:
                score_bf[i] = stage.tile([P, S], BF16, name="score_bf", bufs=12, align_bytes=64)
            bank = psum.tile([P, PACK, P], F32, name="bank")
            q_key = ("q", i // 2)
            for t in range(PACK):
                k_key = ("k", 2 * g + t // 2)
                for j in range(E_PASSES):
                    k_cols = slice(((t % 2) * E_PASSES + j) * P, ((t % 2) * E_PASSES + j + 1) * P)
                    q_cols = slice(((i % 2) * E_PASSES + j) * P, ((i % 2) * E_PASSES + j + 1) * P)
                    nc.tensor.matmul_mx(
                        out=bank[:, t, :],
                        lhsT=codes[k_key][:, k_cols].bitcast(FP8X4),
                        lhsT_scale=scales[k_key][:, k_cols],
                        rhs=codes[q_key][:, q_cols].bitcast(FP8X4),
                        rhs_scale=scales[q_key][:, q_cols],
                        start=(j == 0),
                        stop=(j == E_PASSES - 1),
                    )
            nc.scalar.activation(
                out=score_bf[i][:, g * K_PASS : (g + 1) * K_PASS].rearrange("p (q t) -> p q t", t=PACK),
                in_=bank[:].rearrange("p t q -> p q t"),
                func=ACT.Copy,
                scale=1.0 / math.sqrt(S),
            )

        def quantize_scores(i):
            quantize(("s", i), score_bf[i][:], S // PACK)

        def widen_v(n):
            g, h = divmod(n, HALVES)
            v_rows[n] = stage.tile([P, PACK, BANK], BF16, name="v_rows")
            for t in range(PACK):
                first = t * E + h * BANK
                nc.vector.tensor_scalar(
                    out=v_rows[n][:, t, :],
                    in0=v_bytes[g][:, first : first + BANK].bitcast(FP8),
                    scalar1=v_scale[:, g, t : t + 1],
                    scalar2=None,
                    op0=ALU.mult,
                )

        def weave_v(n):
            v_woven[n] = stage.tile([P, BANK * PACK], BF16, name="v_woven", align_bytes=64)
            nc.vector.tensor_copy(
                out=v_woven[n][:].rearrange("p (c i t) -> p c t i", i=4, t=PACK),
                in_=v_rows[n][:].rearrange("p t (c i) -> p c t i", i=4),
            )

        def quantize_v(n):
            quantize(("v", n), v_woven[n][:], BANK)

        def mix(i, h):
            z_bank[i, h] = psum.tile([P, BANK], F32, name="bank")
            for g in range(S_PASSES):
                cols = slice(g * P, (g + 1) * P)
                v_key = ("v", g * HALVES + h)
                nc.tensor.matmul_mx(
                    out=z_bank[i, h][:],
                    lhsT=codes["s", i][:, cols].bitcast(FP8X4),
                    lhsT_scale=scales["s", i][:, cols],
                    rhs=codes[v_key][:].bitcast(FP8X4),
                    rhs_scale=scales[v_key][:],
                    start=(g == 0),
                    stop=(g == S_PASSES - 1),
                )

        def negate_and_min(i, h):
            if h == 0:
                z_neg[i] = stage.tile([P, E], F32, name="z_neg")
            z_min[i, h] = stage.tile([P, 1], F32, name="z_min", bufs=6)
            nc.vector.tensor_scalar(
                out=z_neg[i][:, h * BANK : (h + 1) * BANK],
                in0=z_bank[i, h][:],
                scalar1=-1.0,
                scalar2=z_min[i, h - 1][:] if h else None,
                op0=ALU.mult,
                op1=ALU.min,
                accum_out=z_min[i, h][:],
            )

        def exponentiate(i):
            expo[i] = stage.tile([P, E], F32, name="expo", tag="raw", bufs=8, align_bytes=256)
            total[i] = stage.tile([P, 1], F32, name="total", bufs=6)
            nc.scalar.activation(
                out=expo[i][:],
                in_=z_neg[i][:],
                func=ACT.Exp,
                scale=-1.0,
                bias=z_min[i, HALVES - 1][:],
                accum_out=total[i][:],
            )

        def invert(i):
            inv[i] = stage.tile([P, 1], F32, name="inv", bufs=6)
            nc.vector.reciprocal(out=inv[i][:], in_=total[i][:])

        def normalize(i, on_vector, share_with_scalar):
            rows = out_tiles[i // 2, i % 2]
            split = (LAST_SPLIT if on_vector else SPLIT) if share_with_scalar else E
            left = expo[i][:, :split]
            if on_vector:
                nc.vector.tensor_scalar(out=left, in0=left, scalar1=inv[i][:], scalar2=None, op0=ALU.mult)
            else:
                nc.gpsimd.tensor_scalar(out=left, in0=left, scalar1=inv[i][:], scalar2=0.0, op0=ALU.mult, op1=ALU.add)
            nc.sync.dma_start(out=rows[:, :split], in_=left)
            if share_with_scalar:
                right = expo[i][:, split:]
                nc.scalar.activation(out=right, in_=right, func=ACT.Copy, scale=inv[i][:])
                nc.sync.dma_start(out=rows[:, split:], in_=right)

        turn_pair(("q", 0), True)
        load_pair(("q", 2))
        turn_pair(("k", 0), True)
        load_pair(("q", 3))
        load_v(1)
        quantize_pair(("q", 0))
        turn_pair(("k", 1), True)
        load_pair(("q", 4))
        quantize_pair(("k", 0))
        turn_pair(("q", 1))
        load_pair(("q", 5))
        load_v(2)
        quantize_pair(("k", 1))
        turn_pair(("k", 2))
        quantize_pair(("q", 1))
        widen_v(0)
        scores(0, 0)
        scores(1, 0)
        quantize_pair(("k", 2))
        widen_v(1)
        turn_pair(("k", 3))
        line_up(("k", 4))
        scores(2, 0)
        scores(3, 0)
        line_up(("k", 5))
        quantize_pair(("k", 3))
        turn_pair(("k", 4))
        turn_pair(("k", 5))
        weave_v(0)
        line_up(("q", 2))
        line_up(("q", 3))
        for i in range(4):
            scores(i, 1)
        quantize_pair(("k", 4))
        quantize_pair(("k", 5))
        turn_pair(("q", 2))
        turn_pair(("q", 3))
        weave_v(1)
        quantize_v(0)
        widen_v(2)
        quantize_pair(("q", 2))
        for i in range(4):
            scores(i, 2)
        quantize_v(1)
        line_up(("q", 4))
        weave_v(2)
        line_up(("q", 5))
        quantize_pair(("q", 3))
        for i in range(4, 6):
            for g in range(S_PASSES):
                scores(i, g)
        turn_pair(("q", 4))
        turn_pair(("q", 5))
        widen_v(3)
        quantize_v(2)
        weave_v(3)
        widen_v(4)
        quantize_pair(("q", 4))
        quantize_v(3)
        quantize_pair(("q", 5))
        weave_v(4)
        widen_v(5)
        quantize_v(4)
        weave_v(5)
        quantize_scores(0)
        quantize_v(5)
        for i in range(6, 11):
            for g in range(S_PASSES):
                scores(i, g)
        quantize_scores(1)

        todo = [(i, g) for i in range(11, TILES) for g in range(S_PASSES)]
        for n in range(2, 4):
            quantize_scores(n)
        quantized, normalized = 4, 0
        for i in range(TILES):
            mix(i, 0)
            mix(i, 1)
            negate_and_min(i, 0)
            for n in range(quantized, min(quantized + (2 if i < len(todo) else 1), TILES)):
                quantize_scores(n)
                quantized = n + 1
            if i >= 2 and normalized == i - 2:
                invert(i - 2)
            negate_and_min(i, 1)
            for n, g in todo[i : i + 1]:
                scores(n, g)
            exponentiate(i)
            for n in range(normalized, i - 1 if i < 9 else i):
                if n == i - 1:
                    invert(n)
                normalize(n, n >= TILES - 2, n < TILES - 2)
                normalized = n + 1
        invert(TILES - 1)
        normalize(TILES - 1, True, True)
